import numpy as np
import ml_dtypes

BF16 = ml_dtypes.bfloat16


def bf(x):
    return np.asarray(x, np.float32).astype(BF16)


def f32(x):
    return np.asarray(x, np.float32)


def f64(x):
    return np.asarray(x).astype(np.float64)


def striped(idx):
    return np.tile(idx.reshape(-1, 16).T, (8, 1))


S, KD, M, HD, REP, D, N = 256, 128, 128, 64, 2, 256, 512


def setup_inputs():
    return {
        "table": bf(np.random.standard_normal((KD, S))),
        "w_tok": bf(np.random.standard_normal((KD, M)) / np.sqrt(D)),
        "pos": bf(np.random.standard_normal((KD, N))),
        "w_pos": bf(np.random.standard_normal((KD, M)) / np.sqrt(D)),
        "b_v": f32(0.1 * np.random.standard_normal((M, 1))),
        "w_o": bf(np.random.standard_normal((D, D)) / np.sqrt(D)),
        "b_o": f32(0.1 * np.random.standard_normal((D, 1))),
        "offs": striped(np.random.permutation(np.tile(np.arange(S), 2))[:N]),
    }


def reference(table, w_tok, pos, w_pos, b_v, w_o, b_o, offs):
    idx = offs[:16].T.reshape(-1)
    v = f64(w_tok).T @ f64(table)[:, idx] + f64(w_pos).T @ f64(pos) + f64(b_v)
    att = np.repeat(v.reshape(M // HD, HD, N), REP, axis=0).reshape(D, N)
    return f64(w_o).T @ att + f64(b_o)

@@ -1,0 +1,75 @@
+import concourse.mybir as mybir
+
+BF16, F32, U16 = mybir.dt.bfloat16, mybir.dt.float32, mybir.dt.uint16
+IDENTITY = mybir.ActivationFunctionType.Identity
+
+P = 128
+WORDS = 256
+N = 512
+PIECE = 256
+HEAD = 64
+REP = 2
+GROUPS = P // HEAD
+D_OUT = 256
+FLOPS = 2 * N * (2 * P * P + GROUPS * REP * HEAD * D_OUT)
+
+
+def add_bias(nc, turn, out, in_, bias):
+    if turn % 2 == 0:
+        nc.vector.tensor_scalar_add(out, in_, bias)
+    else:
+        nc.scalar.activation(out, in_, IDENTITY, bias=bias)
+
+
+def tile_mytransformer_kernel(tc, table, w_tok, pos, w_pos, b_v, w_o, b_o, offs, out):
+    nc = tc.nc
+    with (
+        tc.tile_pool(name="held", bufs=1) as held,
+        tc.tile_pool(name="work", bufs=1) as work,
+        tc.psum_pool(name="psum", bufs=1) as psum,
+    ):
+        offsets = held.tile([P, N // 16], U16, name="offsets")
+        nc.sync.dma_start(offsets[:], offs)
+        table_sb = held.tile([P, WORDS], BF16, name="table_sb")
+        nc.sync.dma_start(table_sb[:], table)
+        w_tok_sb = held.tile([P, P], BF16, name="w_tok_sb")
+        nc.sync.dma_start(w_tok_sb[:], w_tok)
+
+        pos_sb = held.tile([P, N], BF16, name="pos_sb")
+        nc.scalar.dma_start(pos_sb[:], pos)
+        w_pos_sb = held.tile([P, P], BF16, name="w_pos_sb")
+        nc.scalar.dma_start(w_pos_sb[:], w_pos)
+        b_v_sb = held.tile([P, 1], F32, name="b_v_sb")
+        nc.scalar.dma_start(b_v_sb[:], b_v)
+
+        w_o_sb = held.tile([P, REP, D_OUT], BF16, name="w_o_sb")
+        for g, queue in zip(range(GROUPS), (nc.sync, nc.scalar)):
+            queue.dma_start(
+                w_o_sb[g * HEAD : (g + 1) * HEAD, :, :],
+                w_o[g * REP * HEAD : (g + 1) * REP * HEAD, :].rearrange("(r m) o -> m r o", r=REP),
+            )
+        b_o_sb = held.tile([P, D_OUT // P], F32, name="b_o_sb")
+        with nc.allow_non_contiguous_dma(reason="a bias of 256 numbers, one to a partition and block"):
+            nc.sync.dma_start(b_o_sb[:], b_o.rearrange("(ob p) one -> p (ob one)", p=P))
+
+        v_ps = [psum.tile([P, PIECE], F32, name=f"v_ps{h}") for h in range(N // PIECE)]
+        for h in range(N // PIECE):
+            looked_up = table_sb[:].indirect(offsets[:, h * (PIECE // 16) : (h + 1) * (PIECE // 16)])
+            nc.tensor.matmul(v_ps[h][:], w_tok_sb[:], looked_up, start=True, stop=False)
+
+        v_bf = [work.tile([P, PIECE], BF16, name=f"v_bf{h}") for h in range(N // PIECE)]
+        for h in range(N // PIECE):
+            nc.tensor.matmul(v_ps[h][:], w_pos_sb[:], pos_sb[:, h * PIECE : (h + 1) * PIECE], start=False, stop=True)
+            add_bias(nc, h, v_bf[h][:], v_ps[h][:], b_v_sb[:])
+
+        for h in range(N // PIECE):
+            cols = slice(h * PIECE, (h + 1) * PIECE)
+            for ob in range(D_OUT // P):
+                out_ps = psum.tile([P, PIECE], F32, name=f"out_ps{h}_{ob}")
+                for r in range(REP):
+                    nc.tensor.matmul(
+                        out_ps[:], w_o_sb[:, r, ob * P : (ob + 1) * P], v_bf[h][:], start=(r == 0), stop=(r == REP - 1)
+                    )
+                out_sb = work.tile([P, PIECE], F32, name=f"out_sb{h}_{ob}")
+                add_bias(nc, ob, out_sb[:], out_ps[:], b_o_sb[:, ob : ob + 1])
+                nc.sync.dma_start(out[ob * P : (ob + 1) * P, cols], out_sb[:])

@@ -11,6 +11,7 @@ HEAD = 64
 REP = 2
 GROUPS = P // HEAD
 D_OUT = 256
+WARM_UPS = 5
 FLOPS = 2 * N * (2 * P * P + GROUPS * REP * HEAD * D_OUT)
 
 
@@ -51,6 +52,12 @@ def tile_mytransformer_kernel(tc, table, w_tok, pos, w_pos, b_v, w_o, b_o, offs,
         b_o_sb = held.tile([P, D_OUT // P], F32, name="b_o_sb")
         with nc.allow_non_contiguous_dma(reason="a bias of 256 numbers, one to a partition and block"):
             nc.sync.dma_start(b_o_sb[:], b_o.rearrange("(ob p) one -> p (ob one)", p=P))
+
+        zeros = held.tile([P, N], BF16, name="zeros")
+        nc.vector.memset(zeros[:], 0.0)
+        warm_ps = psum.tile([P, N], F32, name="warm_ps")
+        for warm_up in range(WARM_UPS):
+            nc.tensor.matmul(warm_ps[:], zeros[:, 0:P], zeros[:], start=True, stop=True)
 
         v_ps = [psum.tile([P, PIECE], F32, name=f"v_ps{h}") for h in range(N // PIECE)]
         for h in range(N // PIECE):

@@ -11,7 +11,7 @@ HEAD = 64
 REP = 2
 GROUPS = P // HEAD
 D_OUT = 256
-WARM_UPS = 5
+WARM_UPS = 16
 FLOPS = 2 * N * (2 * P * P + GROUPS * REP * HEAD * D_OUT)
 
 
@@ -53,11 +53,13 @@ def tile_mytransformer_kernel(tc, table, w_tok, pos, w_pos, b_v, w_o, b_o, offs,
         with nc.allow_non_contiguous_dma(reason="a bias of 256 numbers, one to a partition and block"):
             nc.sync.dma_start(b_o_sb[:], b_o.rearrange("(ob p) one -> p (ob one)", p=P))
 
-        zeros = held.tile([P, N], BF16, name="zeros")
+        zeros = held.tile([P, P], BF16, name="zeros")
         nc.vector.memset(zeros[:], 0.0)
-        warm_ps = psum.tile([P, N], F32, name="warm_ps")
+        warm_ps = psum.tile([P, P], F32, name="warm_ps")
         for warm_up in range(WARM_UPS):
-            nc.tensor.matmul(warm_ps[:], zeros[:, 0:P], zeros[:], start=True, stop=True)
+            nc.tensor.matmul(warm_ps[:], zeros[:], zeros[:], start=True, stop=True)
+        warm_sb = held.tile([P, 1], F32, name="warm_sb")
+        nc.scalar.activation(warm_sb[:], zeros[:, 0:1], IDENTITY)
 
         v_ps = [psum.tile([P, PIECE], F32, name=f"v_ps{h}") for h in range(N // PIECE)]
         for h in range(N // PIECE):

@@ -63,12 +63,12 @@ def tile_mytransformer_kernel(tc, table, w_tok, pos, w_pos, b_v, w_o, b_o, offs,
 
         v_ps = [psum.tile([P, PIECE], F32, name=f"v_ps{h}") for h in range(N // PIECE)]
         for h in range(N // PIECE):
-            looked_up = table_sb[:].indirect(offsets[:, h * (PIECE // 16) : (h + 1) * (PIECE // 16)])
-            nc.tensor.matmul(v_ps[h][:], w_tok_sb[:], looked_up, start=True, stop=False)
+            nc.tensor.matmul(v_ps[h][:], w_pos_sb[:], pos_sb[:, h * PIECE : (h + 1) * PIECE], start=True, stop=False)
 
         v_bf = [work.tile([P, PIECE], BF16, name=f"v_bf{h}") for h in range(N // PIECE)]
         for h in range(N // PIECE):
-            nc.tensor.matmul(v_ps[h][:], w_pos_sb[:], pos_sb[:, h * PIECE : (h + 1) * PIECE], start=False, stop=True)
+            looked_up = table_sb[:].indirect(offsets[:, h * (PIECE // 16) : (h + 1) * (PIECE // 16)])
+            nc.tensor.matmul(v_ps[h][:], w_tok_sb[:], looked_up, start=False, stop=True)
             add_bias(nc, h, v_bf[h][:], v_ps[h][:], b_v_sb[:])
 
         for h in range(N // PIECE):

@@ -6,12 +6,13 @@ IDENTITY = mybir.ActivationFunctionType.Identity
 P = 128
 WORDS = 256
 N = 512
-PIECE = 256
+HALF = 256
+PIECES = ((0, 128), (128, 128), (256, 256))
 HEAD = 64
 REP = 2
 GROUPS = P // HEAD
 D_OUT = 256
-WARM_UPS = 16
+WARM_UPS = 10
 FLOPS = 2 * N * (2 * P * P + GROUPS * REP * HEAD * D_OUT)
 
 
@@ -61,24 +62,37 @@ def tile_mytransformer_kernel(tc, table, w_tok, pos, w_pos, b_v, w_o, b_o, offs,
         warm_sb = held.tile([P, 1], F32, name="warm_sb")
         nc.scalar.activation(warm_sb[:], zeros[:, 0:1], IDENTITY)
 
-        v_ps = [psum.tile([P, PIECE], F32, name=f"v_ps{h}") for h in range(N // PIECE)]
-        for h in range(N // PIECE):
-            nc.tensor.matmul(v_ps[h][:], w_pos_sb[:], pos_sb[:, h * PIECE : (h + 1) * PIECE], start=True, stop=False)
+        v_ps = [psum.tile([P, entries], F32, name=f"v_ps{first}") for first, entries in PIECES]
 
-        v_bf = [work.tile([P, PIECE], BF16, name=f"v_bf{h}") for h in range(N // PIECE)]
-        for h in range(N // PIECE):
-            looked_up = table_sb[:].indirect(offsets[:, h * (PIECE // 16) : (h + 1) * (PIECE // 16)])
-            nc.tensor.matmul(v_ps[h][:], w_tok_sb[:], looked_up, start=False, stop=True)
-            add_bias(nc, h, v_bf[h][:], v_ps[h][:], b_v_sb[:])
+        def position_half(piece, start):
+            first, entries = PIECES[piece]
+            nc.tensor.matmul(v_ps[piece][:], w_pos_sb[:], pos_sb[:, first : first + entries], start=start, stop=not start)
 
-        for h in range(N // PIECE):
-            cols = slice(h * PIECE, (h + 1) * PIECE)
+        def token_half(piece, start):
+            first, entries = PIECES[piece]
+            looked_up = table_sb[:].indirect(offsets[:, first // 16 : (first + entries) // 16])
+            nc.tensor.matmul(v_ps[piece][:], w_tok_sb[:], looked_up, start=start, stop=not start)
+
+        last = len(PIECES) - 1
+        for piece in range(last):
+            position_half(piece, start=True)
+        for piece in range(last):
+            token_half(piece, start=False)
+        token_half(last, start=True)
+        position_half(last, start=False)
+
+        v_bf = work.tile([P, N], BF16, name="v_bf")
+        for piece, (first, entries) in enumerate(PIECES):
+            add_bias(nc, piece, v_bf[:, first : first + entries], v_ps[piece][:], b_v_sb[:])
+
+        for h in range(N // HALF):
+            cols = slice(h * HALF, (h + 1) * HALF)
             for ob in range(D_OUT // P):
-                out_ps = psum.tile([P, PIECE], F32, name=f"out_ps{h}_{ob}")
+                out_ps = psum.tile([P, HALF], F32, name=f"out_ps{h}_{ob}")
                 for r in range(REP):
                     nc.tensor.matmul(
-                        out_ps[:], w_o_sb[:, r, ob * P : (ob + 1) * P], v_bf[h][:], start=(r == 0), stop=(r == REP - 1)
+                        out_ps[:], w_o_sb[:, r, ob * P : (ob + 1) * P], v_bf[:, cols], start=(r == 0), stop=(r == REP - 1)
                     )
-                out_sb = work.tile([P, PIECE], F32, name=f"out_sb{h}_{ob}")
-                add_bias(nc, ob, out_sb[:], out_ps[:], b_o_sb[:, ob : ob + 1])
+                out_sb = work.tile([P, HALF], F32, name=f"out_sb{h}_{ob}")
+                add_bias(nc, ob + 1, out_sb[:], out_ps[:], b_o_sb[:, ob : ob + 1])
                 nc.sync.dma_start(out[ob * P : (ob + 1) * P, cols], out_sb[:])

@@ -12,7 +12,7 @@ HEAD = 64
 REP = 2
 GROUPS = P // HEAD
 D_OUT = 256
-WARM_UPS = 10
+WARM_UPS = 16
 FLOPS = 2 * N * (2 * P * P + GROUPS * REP * HEAD * D_OUT)
 
 

@@ -30,22 +30,22 @@ def tile_mytransformer_kernel(tc, table, w_tok, pos, w_pos, b_v, w_o, b_o, offs,
         tc.tile_pool(name="work", bufs=1) as work,
         tc.psum_pool(name="psum", bufs=1) as psum,
     ):
+        w_pos_sb = held.tile([P, P], BF16, name="w_pos_sb")
+        nc.sync.dma_start(w_pos_sb[:], w_pos)
+        pos_sb = [held.tile([P, HALF], BF16, name=f"pos_sb{h}") for h in range(N // HALF)]
+        nc.scalar.dma_start(pos_sb[0][:], pos[:, 0:HALF])
         offsets = held.tile([P, N // 16], U16, name="offsets")
         nc.sync.dma_start(offsets[:], offs)
+        w_tok_sb = held.tile([P, P], BF16, name="w_tok_sb")
+        nc.scalar.dma_start(w_tok_sb[:], w_tok)
         table_sb = held.tile([P, WORDS], BF16, name="table_sb")
         nc.sync.dma_start(table_sb[:], table)
-        w_tok_sb = held.tile([P, P], BF16, name="w_tok_sb")
-        nc.sync.dma_start(w_tok_sb[:], w_tok)
-
-        pos_sb = held.tile([P, N], BF16, name="pos_sb")
-        nc.scalar.dma_start(pos_sb[:], pos)
-        w_pos_sb = held.tile([P, P], BF16, name="w_pos_sb")
-        nc.scalar.dma_start(w_pos_sb[:], w_pos)
         b_v_sb = held.tile([P, 1], F32, name="b_v_sb")
         nc.scalar.dma_start(b_v_sb[:], b_v)
+        nc.sync.dma_start(pos_sb[1][:], pos[:, HALF:N])
 
         w_o_sb = held.tile([P, REP, D_OUT], BF16, name="w_o_sb")
-        for g, queue in zip(range(GROUPS), (nc.sync, nc.scalar)):
+        for g, queue in zip(range(GROUPS), (nc.scalar, nc.sync)):
             queue.dma_start(
                 w_o_sb[g * HEAD : (g + 1) * HEAD, :, :],
                 w_o[g * REP * HEAD : (g + 1) * REP * HEAD, :].rearrange("(r m) o -> m r o", r=REP),
@@ -66,7 +66,8 @@ def tile_mytransformer_kernel(tc, table, w_tok, pos, w_pos, b_v, w_o, b_o, offs,
 
         def position_half(piece, start):
             first, entries = PIECES[piece]
-            nc.tensor.matmul(v_ps[piece][:], w_pos_sb[:], pos_sb[:, first : first + entries], start=start, stop=not start)
+            moving = pos_sb[first // HALF][:, first % HALF : first % HALF + entries]
+            nc.tensor.matmul(v_ps[piece][:], w_pos_sb[:], moving, start=start, stop=not start)
 
         def token_half(piece, start):
             first, entries = PIECES[piece]

@@ -12,7 +12,7 @@ HEAD = 64
 REP = 2
 GROUPS = P // HEAD
 D_OUT = 256
-WARM_UPS = 16
+WARM_UPS = 10
 FLOPS = 2 * N * (2 * P * P + GROUPS * REP * HEAD * D_OUT)
 
 

@@ -84,7 +84,7 @@ def tile_mytransformer_kernel(tc, table, w_tok, pos, w_pos, b_v, w_o, b_o, offs,
 
         v_bf = work.tile([P, N], BF16, name="v_bf")
         for piece, (first, entries) in enumerate(PIECES):
-            add_bias(nc, piece, v_bf[:, first : first + entries], v_ps[piece][:], b_v_sb[:])
+            nc.vector.tensor_scalar_add(v_bf[:, first : first + entries], v_ps[piece][:], b_v_sb[:])
 
         for h in range(N // HALF):
             cols = slice(h * HALF, (h + 1) * HALF)

@@ -95,5 +95,5 @@ def tile_mytransformer_kernel(tc, table, w_tok, pos, w_pos, b_v, w_o, b_o, offs,
                         out_ps[:], w_o_sb[:, r, ob * P : (ob + 1) * P], v_bf[:, cols], start=(r == 0), stop=(r == REP - 1)
                     )
                 out_sb = work.tile([P, HALF], F32, name=f"out_sb{h}_{ob}")
-                add_bias(nc, ob + 1, out_sb[:], out_ps[:], b_o_sb[:, ob : ob + 1])
+                add_bias(nc, ob, out_sb[:], out_ps[:], b_o_sb[:, ob : ob + 1])
                 nc.sync.dma_start(out[ob * P : (ob + 1) * P, cols], out_sb[:])

@@ -30,12 +30,12 @@ def tile_mytransformer_kernel(tc, table, w_tok, pos, w_pos, b_v, w_o, b_o, offs,
         tc.tile_pool(name="work", bufs=1) as work,
         tc.psum_pool(name="psum", bufs=1) as psum,
     ):
-        w_pos_sb = held.tile([P, P], BF16, name="w_pos_sb")
-        nc.sync.dma_start(w_pos_sb[:], w_pos)
-        pos_sb = [held.tile([P, HALF], BF16, name=f"pos_sb{h}") for h in range(N // HALF)]
-        nc.scalar.dma_start(pos_sb[0][:], pos[:, 0:HALF])
         offsets = held.tile([P, N // 16], U16, name="offsets")
         nc.sync.dma_start(offsets[:], offs)
+        pos_sb = [held.tile([P, HALF], BF16, name=f"pos_sb{h}") for h in range(N // HALF)]
+        nc.scalar.dma_start(pos_sb[0][:], pos[:, 0:HALF])
+        w_pos_sb = held.tile([P, P], BF16, name="w_pos_sb")
+        nc.sync.dma_start(w_pos_sb[:], w_pos)
         w_tok_sb = held.tile([P, P], BF16, name="w_tok_sb")
         nc.scalar.dma_start(w_tok_sb[:], w_tok)
         table_sb = held.tile([P, WORDS], BF16, name="table_sb")

import concourse.mybir as mybir

BF16, F32, U16 = mybir.dt.bfloat16, mybir.dt.float32, mybir.dt.uint16
IDENTITY = mybir.ActivationFunctionType.Identity

P = 128
WORDS = 256
N = 512
HALF = 256
PIECES = ((0, 128), (128, 128), (256, 256))
HEAD = 64
REP = 2
GROUPS = P // HEAD
D_OUT = 256
WARM_UPS = 10
FLOPS = 2 * N * (2 * P * P + GROUPS * REP * HEAD * D_OUT)


def add_bias(nc, turn, out, in_, bias):
    if turn % 2 == 0:
        nc.vector.tensor_scalar_add(out, in_, bias)
    else:
        nc.scalar.activation(out, in_, IDENTITY, bias=bias)


def tile_mytransformer_kernel(tc, table, w_tok, pos, w_pos, b_v, w_o, b_o, offs, out):
    nc = tc.nc
    with (
        tc.tile_pool(name="held", bufs=1) as held,
        tc.tile_pool(name="work", bufs=1) as work,
        tc.psum_pool(name="psum", bufs=1) as psum,
    ):
        offsets = held.tile([P, N // 16], U16, name="offsets")
        nc.sync.dma_start(offsets[:], offs)
        pos_sb = [held.tile([P, HALF], BF16, name=f"pos_sb{h}") for h in range(N // HALF)]
        nc.scalar.dma_start(pos_sb[0][:], pos[:, 0:HALF])
        w_pos_sb = held.tile([P, P], BF16, name="w_pos_sb")
        nc.sync.dma_start(w_pos_sb[:], w_pos)
        w_tok_sb = held.tile([P, P], BF16, name="w_tok_sb")
        nc.scalar.dma_start(w_tok_sb[:], w_tok)
        table_sb = held.tile([P, WORDS], BF16, name="table_sb")
        nc.sync.dma_start(table_sb[:], table)
        b_v_sb = held.tile([P, 1], F32, name="b_v_sb")
        nc.scalar.dma_start(b_v_sb[:], b_v)
        nc.sync.dma_start(pos_sb[1][:], pos[:, HALF:N])

        w_o_sb = held.tile([P, REP, D_OUT], BF16, name="w_o_sb")
        for g, queue in zip(range(GROUPS), (nc.scalar, nc.sync)):
            queue.dma_start(
                w_o_sb[g * HEAD : (g + 1) * HEAD, :, :],
                w_o[g * REP * HEAD : (g + 1) * REP * HEAD, :].rearrange("(r m) o -> m r o", r=REP),
            )
        b_o_sb = held.tile([P, D_OUT // P], F32, name="b_o_sb")
        with nc.allow_non_contiguous_dma(reason="a bias of 256 numbers, one to a partition and block"):
            nc.sync.dma_start(b_o_sb[:], b_o.rearrange("(ob p) one -> p (ob one)", p=P))

        zeros = held.tile([P, P], BF16, name="zeros")
        nc.vector.memset(zeros[:], 0.0)
        warm_ps = psum.tile([P, P], F32, name="warm_ps")
        for warm_up in range(WARM_UPS):
            nc.tensor.matmul(warm_ps[:], zeros[:], zeros[:], start=True, stop=True)
        warm_sb = held.tile([P, 1], F32, name="warm_sb")
        nc.scalar.activation(warm_sb[:], zeros[:, 0:1], IDENTITY)

        v_ps = [psum.tile([P, entries], F32, name=f"v_ps{first}") for first, entries in PIECES]

        def position_half(piece, start):
            first, entries = PIECES[piece]
            moving = pos_sb[first // HALF][:, first % HALF : first % HALF + entries]
            nc.tensor.matmul(v_ps[piece][:], w_pos_sb[:], moving, start=start, stop=not start)

        def token_half(piece, start):
            first, entries = PIECES[piece]
            looked_up = table_sb[:].indirect(offsets[:, first // 16 : (first + entries) // 16])
            nc.tensor.matmul(v_ps[piece][:], w_tok_sb[:], looked_up, start=start, stop=not start)

        last = len(PIECES) - 1
        for piece in range(last):
            position_half(piece, start=True)
        for piece in range(last):
            token_half(piece, start=False)
        token_half(last, start=True)
        position_half(last, start=False)

        v_bf = work.tile([P, N], BF16, name="v_bf")
        for piece, (first, entries) in enumerate(PIECES):
            nc.vector.tensor_scalar_add(v_bf[:, first : first + entries], v_ps[piece][:], b_v_sb[:])

        for h in range(N // HALF):
            cols = slice(h * HALF, (h + 1) * HALF)
            for ob in range(D_OUT // P):
                out_ps = psum.tile([P, HALF], F32, name=f"out_ps{h}_{ob}")
                for r in range(REP):
                    nc.tensor.matmul(
                        out_ps[:], w_o_sb[:, r, ob * P : (ob + 1) * P], v_bf[:, cols], start=(r == 0), stop=(r == REP - 1)
                    )
                out_sb = work.tile([P, HALF], F32, name=f"out_sb{h}_{ob}")
                add_bias(nc, ob, out_sb[:], out_ps[:], b_o_sb[:, ob : ob + 1])
                nc.sync.dma_start(out[ob * P : (ob + 1) * P, cols], out_sb[:])
